import numpy as np
import ml_dtypes

BF16 = ml_dtypes.bfloat16


def bf(x):
    return np.asarray(x, np.float32).astype(BF16)


def f32(x):
    return np.asarray(x, np.float32)


def f64(x):
    return np.asarray(x).astype(np.float64)


def striped(idx):
    return np.tile(idx.reshape(-1, 16).T, (8, 1))


S, D, M, N = 512, 128, 256, 256


def setup_inputs():
    return {"q": bf(np.random.standard_normal((D, M))), "table": bf(np.random.standard_normal((S, D))), "k_scale": f32(np.random.uniform(1.0, 2.0, (1, N))), "v": bf(np.random.standard_normal((N, D))), "offs": striped(np.random.permutation(S)[:N])}


def reference(q, table, k_scale, v, offs):
    idx = offs[:16].T.reshape(-1)
    sc = (f64(q).T @ f64(table)[idx].T) * f64(k_scale) / np.sqrt(D)
    keep = np.arange(N)[None, :] <= np.arange(M)[:, None]
    sc = np.where(keep, sc, -np.inf)
    e = np.exp(sc - sc.max(axis=1, keepdims=True))
    a = e / e.sum(axis=1, keepdims=True)
    return a @ f64(v)

@@ -1,0 +1,113 @@
+import math
+
+import concourse.mybir as mybir
+from concourse.masks import make_identity
+
+S, D, M, N = 512, 128, 256, 256
+P = 128
+SLOT_BLOCKS, QUERY_BLOCKS, KEY_BLOCKS = S // P, M // P, N // P
+MASKED = -1.0e30
+
+FLOPS = 2 * 2 * D * (M * (M + 1) // 2)
+
+BF16, F32, U16 = mybir.dt.bfloat16, mybir.dt.float32, mybir.dt.uint16
+ALU = mybir.AluOpType
+ACT = mybir.ActivationFunctionType
+
+
+def tile_pagedattention_kernel(tc, q, table, k_scale, v, offs, out):
+    nc = tc.nc
+    with (
+        tc.tile_pool(name="held", bufs=1) as held,
+        tc.tile_pool(name="work", bufs=2) as work,
+        tc.psum_pool(name="psum", bufs=2) as psum,
+    ):
+        offsets = held.tile([P, N // 16], U16, name="offsets")
+        nc.sync.dma_start(offsets[:], offs)
+
+        table_rows = held.tile([P, SLOT_BLOCKS, D], BF16, name="table_rows")
+        table_blocks = table.rearrange("(b p) d -> p b d", p=P)
+        nc.sync.dma_start(table_rows[:, 0:2, :], table_blocks[:, 0:2, :])
+        nc.scalar.dma_start(table_rows[:, 2:4, :], table_blocks[:, 2:4, :])
+
+        q_cols = held.tile([D, M], BF16, name="q_cols")
+        nc.sync.dma_start(q_cols[:], q)
+        key_scale_raw = held.tile([P, N], F32, name="key_scale_raw")
+        nc.scalar.dma_start(key_scale_raw[:], k_scale.rearrange("o n -> (o n)").partition_broadcast(P))
+        v_rows = held.tile([P, KEY_BLOCKS, D], BF16, name="v_rows")
+        nc.gpsimd.dma_start(v_rows[:], v.rearrange("(b p) e -> p b e", p=P))
+
+        warm = held.tile([P, 1], F32, name="warm")
+        warmed = held.tile([P, 1], F32, name="warmed")
+        nc.vector.memset(warm[:], 0.0)
+        nc.scalar.activation(warmed[:], warm[:], ACT.Exp)
+
+        identity = held.tile([P, P], BF16, name="identity")
+        make_identity(nc, identity[:])
+
+        causal_bias = held.tile([P, P], F32, name="causal_bias")
+        nc.gpsimd.memset(causal_bias[:], 0.0)
+        nc.gpsimd.affine_select(
+            out=causal_bias[:],
+            in_=causal_bias[:],
+            pattern=[[-1, P]],
+            compare_op=ALU.is_ge,
+            fill=MASKED,
+            base=0,
+            channel_multiplier=1,
+        )
+
+        key_scale = held.tile([P, N], F32, name="key_scale")
+        nc.vector.tensor_scalar_mul(key_scale[:], key_scale_raw[:], 1.0 / math.sqrt(D))
+
+        table_cols = held.tile([D, S], BF16, name="table_cols")
+        for half in range(2):
+            flipped = psum.tile([D, 2 * P], BF16, name="flipped")
+            for k in range(2):
+                nc.tensor.transpose(flipped[:, k * P : (k + 1) * P], table_rows[:, 2 * half + k, :], identity[:])
+            if half == 0:
+                nc.vector.tensor_copy(table_cols[:, 0 : 2 * P], flipped[:])
+            else:
+                nc.scalar.copy(table_cols[:, 2 * P : 4 * P], flipped[:])
+
+        for i in reversed(range(QUERY_BLOCKS)):
+            keys = (i + 1) * P
+            rows = slice(i * P, (i + 1) * P)
+
+            scores_ps = psum.tile([P, N], F32, name="scores_ps")
+            nc.tensor.matmul(
+                scores_ps[:, :keys],
+                q_cols[:, rows],
+                table_cols[:].indirect(offsets[:, : keys // 16]),
+                start=True,
+                stop=True,
+            )
+
+            scores = work.tile([P, N], F32, name="scores")
+            nc.vector.tensor_tensor(scores[:, :keys], scores_ps[:, :keys], key_scale[:, :keys], ALU.mult)
+            nc.vector.tensor_tensor(scores[:, rows], scores[:, rows], causal_bias[:], ALU.add)
+            neg_max = work.tile([P, 1], F32, name="neg_max")
+            nc.vector.reduce_max(neg_max[:], scores[:, :keys], axis=mybir.AxisListType.X, negate=True)
+
+            weights = work.tile([P, N], BF16, name="weights")
+            row_sum = work.tile([P, 1], F32, name="row_sum")
+            nc.scalar.activation(
+                weights[:, :keys], scores[:, :keys], ACT.Exp, bias=neg_max[:], scale=1.0, accum_out=row_sum[:]
+            )
+            inv_sum = work.tile([P, 1], F32, name="inv_sum")
+            nc.vector.reciprocal(inv_sum[:], row_sum[:])
+
+            weights_flipped_ps = psum.tile([P, N], BF16, name="weights_flipped_ps")
+            for b in range(i + 1):
+                nc.tensor.transpose(weights_flipped_ps[:, b * P : (b + 1) * P], weights[:, b * P : (b + 1) * P], identity[:])
+            weights_flipped = work.tile([P, N], BF16, name="weights_flipped")
+            nc.vector.tensor_copy(weights_flipped[:, :keys], weights_flipped_ps[:, :keys])
+
+            out_ps = psum.tile([P, D], F32, name="out_ps")
+            for b in range(i + 1):
+                nc.tensor.matmul(
+                    out_ps[:], weights_flipped[:, b * P : (b + 1) * P], v_rows[:, b, :], start=(b == 0), stop=(b == i)
+                )
+            out_rows = work.tile([P, D], F32, name="out_rows")
+            nc.vector.tensor_scalar_mul(out_rows[:], out_ps[:], inv_sum[:])
+            nc.sync.dma_start(out[rows, :], out_rows[:])

@@ -22,20 +22,19 @@ def tile_pagedattention_kernel(tc, q, table, k_scale, v, offs, out):
         tc.tile_pool(name="work", bufs=2) as work,
         tc.psum_pool(name="psum", bufs=2) as psum,
     ):
-        offsets = held.tile([P, N // 16], U16, name="offsets")
-        nc.sync.dma_start(offsets[:], offs)
-
         table_rows = held.tile([P, SLOT_BLOCKS, D], BF16, name="table_rows")
         table_blocks = table.rearrange("(b p) d -> p b d", p=P)
         nc.sync.dma_start(table_rows[:, 0:2, :], table_blocks[:, 0:2, :])
         nc.scalar.dma_start(table_rows[:, 2:4, :], table_blocks[:, 2:4, :])
 
+        offsets = held.tile([P, N // 16], U16, name="offsets")
+        nc.sync.dma_start(offsets[:], offs)
         q_cols = held.tile([D, M], BF16, name="q_cols")
         nc.sync.dma_start(q_cols[:], q)
         key_scale_raw = held.tile([P, N], F32, name="key_scale_raw")
         nc.scalar.dma_start(key_scale_raw[:], k_scale.rearrange("o n -> (o n)").partition_broadcast(P))
         v_rows = held.tile([P, KEY_BLOCKS, D], BF16, name="v_rows")
-        nc.gpsimd.dma_start(v_rows[:], v.rearrange("(b p) e -> p b e", p=P))
+        nc.sync.dma_start(v_rows[:], v.rearrange("(b p) e -> p b e", p=P))
 
         warm = held.tile([P, 1], F32, name="warm")
         warmed = held.tile([P, 1], F32, name="warmed")
@@ -43,10 +42,11 @@ def tile_pagedattention_kernel(tc, q, table, k_scale, v, offs, out):
         nc.scalar.activation(warmed[:], warm[:], ACT.Exp)
 
         identity = held.tile([P, P], BF16, name="identity")
-        make_identity(nc, identity[:])
+        nc.vector.memset(identity[:], 0.0)
+        make_identity(nc, identity[:], nomemset=True)
 
         causal_bias = held.tile([P, P], F32, name="causal_bias")
-        nc.gpsimd.memset(causal_bias[:], 0.0)
+        nc.vector.memset(causal_bias[:], 0.0)
         nc.gpsimd.affine_select(
             out=causal_bias[:],
             in_=causal_bias[:],

@@ -19,8 +19,8 @@ def tile_pagedattention_kernel(tc, q, table, k_scale, v, offs, out):
     nc = tc.nc
     with (
         tc.tile_pool(name="held", bufs=1) as held,
-        tc.tile_pool(name="work", bufs=2) as work,
-        tc.psum_pool(name="psum", bufs=2) as psum,
+        tc.tile_pool(name="work", bufs=1) as work,
+        tc.psum_pool(name="psum", bufs=1) as psum,
     ):
         table_rows = held.tile([P, SLOT_BLOCKS, D], BF16, name="table_rows")
         table_blocks = table.rearrange("(b p) d -> p b d", p=P)
@@ -62,7 +62,7 @@ def tile_pagedattention_kernel(tc, q, table, k_scale, v, offs, out):
 
         table_cols = held.tile([D, S], BF16, name="table_cols")
         for half in range(2):
-            flipped = psum.tile([D, 2 * P], BF16, name="flipped")
+            flipped = psum.tile([D, 2 * P], BF16, name=f"flipped{half}")
             for k in range(2):
                 nc.tensor.transpose(flipped[:, k * P : (k + 1) * P], table_rows[:, 2 * half + k, :], identity[:])
             if half == 0:
@@ -70,44 +70,53 @@ def tile_pagedattention_kernel(tc, q, table, k_scale, v, offs, out):
             else:
                 nc.scalar.copy(table_cols[:, 2 * P : 4 * P], flipped[:])
 
-        for i in reversed(range(QUERY_BLOCKS)):
-            keys = (i + 1) * P
-            rows = slice(i * P, (i + 1) * P)
+        blocks = list(reversed(range(QUERY_BLOCKS)))
+        keys = [(i + 1) * P for i in range(QUERY_BLOCKS)]
+        rows = [slice(i * P, (i + 1) * P) for i in range(QUERY_BLOCKS)]
 
-            scores_ps = psum.tile([P, N], F32, name="scores_ps")
+        scores_ps = [psum.tile([P, keys[i]], F32, name=f"scores_ps{i}") for i in range(QUERY_BLOCKS)]
+        for i in blocks:
             nc.tensor.matmul(
-                scores_ps[:, :keys],
-                q_cols[:, rows],
-                table_cols[:].indirect(offsets[:, : keys // 16]),
+                scores_ps[i][:],
+                q_cols[:, rows[i]],
+                table_cols[:].indirect(offsets[:, : keys[i] // 16]),
                 start=True,
                 stop=True,
             )
 
-            scores = work.tile([P, N], F32, name="scores")
-            nc.vector.tensor_tensor(scores[:, :keys], scores_ps[:, :keys], key_scale[:, :keys], ALU.mult)
-            nc.vector.tensor_tensor(scores[:, rows], scores[:, rows], causal_bias[:], ALU.add)
-            neg_max = work.tile([P, 1], F32, name="neg_max")
-            nc.vector.reduce_max(neg_max[:], scores[:, :keys], axis=mybir.AxisListType.X, negate=True)
+        scores = [work.tile([P, keys[i]], F32, name=f"scores{i}") for i in range(QUERY_BLOCKS)]
+        neg_max = [work.tile([P, 1], F32, name=f"neg_max{i}") for i in range(QUERY_BLOCKS)]
+        for i in blocks:
+            nc.vector.tensor_tensor(scores[i][:], scores_ps[i][:], key_scale[:, : keys[i]], ALU.mult)
+        for i in blocks:
+            nc.vector.tensor_tensor(scores[i][:, rows[i]], scores[i][:, rows[i]], causal_bias[:], ALU.add)
+        for i in blocks:
+            nc.vector.reduce_max(neg_max[i][:], scores[i][:], axis=mybir.AxisListType.X, negate=True)
 
-            weights = work.tile([P, N], BF16, name="weights")
-            row_sum = work.tile([P, 1], F32, name="row_sum")
+        weights = [work.tile([P, keys[i]], BF16, name=f"weights{i}") for i in range(QUERY_BLOCKS)]
+        row_sum = [work.tile([P, 1], F32, name=f"row_sum{i}") for i in range(QUERY_BLOCKS)]
+        inv_sum = [work.tile([P, 1], F32, name=f"inv_sum{i}") for i in range(QUERY_BLOCKS)]
+        for i in blocks:
             nc.scalar.activation(
-                weights[:, :keys], scores[:, :keys], ACT.Exp, bias=neg_max[:], scale=1.0, accum_out=row_sum[:]
+                weights[i][:], scores[i][:], ACT.Exp, bias=neg_max[i][:], scale=1.0, accum_out=row_sum[i][:]
             )
-            inv_sum = work.tile([P, 1], F32, name="inv_sum")
-            nc.vector.reciprocal(inv_sum[:], row_sum[:])
+        for i in blocks:
+            nc.vector.reciprocal(inv_sum[i][:], row_sum[i][:])
 
-            weights_flipped_ps = psum.tile([P, N], BF16, name="weights_flipped_ps")
+        weights_flipped_ps = [psum.tile([P, keys[i]], BF16, name=f"weights_flipped_ps{i}") for i in range(QUERY_BLOCKS)]
+        weights_flipped = [work.tile([P, keys[i]], BF16, name=f"weights_flipped{i}") for i in range(QUERY_BLOCKS)]
+        for i in blocks:
             for b in range(i + 1):
-                nc.tensor.transpose(weights_flipped_ps[:, b * P : (b + 1) * P], weights[:, b * P : (b + 1) * P], identity[:])
-            weights_flipped = work.tile([P, N], BF16, name="weights_flipped")
-            nc.vector.tensor_copy(weights_flipped[:, :keys], weights_flipped_ps[:, :keys])
+                nc.tensor.transpose(weights_flipped_ps[i][:, rows[b]], weights[i][:, rows[b]], identity[:])
+        nc.vector.tensor_copy(weights_flipped[1][:], weights_flipped_ps[1][:])
+        nc.scalar.copy(weights_flipped[0][:], weights_flipped_ps[0][:])
 
-            out_ps = psum.tile([P, D], F32, name="out_ps")
+        out_ps = [psum.tile([P, D], F32, name=f"out_ps{i}") for i in range(QUERY_BLOCKS)]
+        out_rows = [work.tile([P, D], F32, name=f"out_rows{i}") for i in range(QUERY_BLOCKS)]
+        for i in blocks:
             for b in range(i + 1):
-                nc.tensor.matmul(
-                    out_ps[:], weights_flipped[:, b * P : (b + 1) * P], v_rows[:, b, :], start=(b == 0), stop=(b == i)
-                )
-            out_rows = work.tile([P, D], F32, name="out_rows")
-            nc.vector.tensor_scalar_mul(out_rows[:], out_ps[:], inv_sum[:])
-            nc.sync.dma_start(out[rows, :], out_rows[:])
+                nc.tensor.matmul(out_ps[i][:], weights_flipped[i][:, rows[b]], v_rows[:, b, :], start=(b == 0), stop=(b == i))
+        nc.vector.tensor_scalar_mul(out_rows[1][:], out_ps[1][:], inv_sum[1][:])
+        nc.sync.dma_start(out[rows[1], :], out_rows[1][:])
+        nc.scalar.mul(out_rows[0][:], out_ps[0][:], inv_sum[0][:])
+        nc.scalar.dma_start(out[rows[0], :], out_rows[0][:])

@@ -19,8 +19,8 @@ def tile_pagedattention_kernel(tc, q, table, k_scale, v, offs, out):
     nc = tc.nc
     with (
         tc.tile_pool(name="held", bufs=1) as held,
-        tc.tile_pool(name="work", bufs=1) as work,
-        tc.psum_pool(name="psum", bufs=1) as psum,
+        tc.tile_pool(name="work", bufs=2) as work,
+        tc.psum_pool(name="psum", bufs=2) as psum,
     ):
         table_rows = held.tile([P, SLOT_BLOCKS, D], BF16, name="table_rows")
         table_blocks = table.rearrange("(b p) d -> p b d", p=P)
@@ -62,61 +62,49 @@ def tile_pagedattention_kernel(tc, q, table, k_scale, v, offs, out):
 
         table_cols = held.tile([D, S], BF16, name="table_cols")
         for half in range(2):
-            flipped = psum.tile([D, 2 * P], BF16, name=f"flipped{half}")
+            flipped = psum.tile([D, 2 * P], BF16, name="flipped")
             for k in range(2):
                 nc.tensor.transpose(flipped[:, k * P : (k + 1) * P], table_rows[:, 2 * half + k, :], identity[:])
-            if half == 0:
-                nc.vector.tensor_copy(table_cols[:, 0 : 2 * P], flipped[:])
-            else:
-                nc.scalar.copy(table_cols[:, 2 * P : 4 * P], flipped[:])
+            nc.vector.tensor_copy(table_cols[:, 2 * half * P : 2 * (half + 1) * P], flipped[:])
 
-        blocks = list(reversed(range(QUERY_BLOCKS)))
-        keys = [(i + 1) * P for i in range(QUERY_BLOCKS)]
-        rows = [slice(i * P, (i + 1) * P) for i in range(QUERY_BLOCKS)]
+        for i in reversed(range(QUERY_BLOCKS)):
+            keys = (i + 1) * P
+            rows = slice(i * P, (i + 1) * P)
 
-        scores_ps = [psum.tile([P, keys[i]], F32, name=f"scores_ps{i}") for i in range(QUERY_BLOCKS)]
-        for i in blocks:
+            scores_ps = psum.tile([P, N], F32, name="scores_ps")
             nc.tensor.matmul(
-                scores_ps[i][:],
-                q_cols[:, rows[i]],
-                table_cols[:].indirect(offsets[:, : keys[i] // 16]),
+                scores_ps[:, :keys],
+                q_cols[:, rows],
+                table_cols[:].indirect(offsets[:, : keys // 16]),
                 start=True,
                 stop=True,
             )
 
-        scores = [work.tile([P, keys[i]], F32, name=f"scores{i}") for i in range(QUERY_BLOCKS)]
-        neg_max = [work.tile([P, 1], F32, name=f"neg_max{i}") for i in range(QUERY_BLOCKS)]
-        for i in blocks:
-            nc.vector.tensor_tensor(scores[i][:], scores_ps[i][:], key_scale[:, : keys[i]], ALU.mult)
-        for i in blocks:
-            nc.vector.tensor_tensor(scores[i][:, rows[i]], scores[i][:, rows[i]], causal_bias[:], ALU.add)
-        for i in blocks:
-            nc.vector.reduce_max(neg_max[i][:], scores[i][:], axis=mybir.AxisListType.X, negate=True)
+            scores = work.tile([P, N], F32, name="scores")
+            nc.vector.tensor_tensor(scores[:, :keys], scores_ps[:, :keys], key_scale[:, :keys], ALU.mult)
+            nc.vector.tensor_tensor(scores[:, rows], scores[:, rows], causal_bias[:], ALU.add)
+            neg_max = work.tile([P, 1], F32, name="neg_max")
+            nc.vector.reduce_max(neg_max[:], scores[:, :keys], axis=mybir.AxisListType.X, negate=True)
 
-        weights = [work.tile([P, keys[i]], BF16, name=f"weights{i}") for i in range(QUERY_BLOCKS)]
-        row_sum = [work.tile([P, 1], F32, name=f"row_sum{i}") for i in range(QUERY_BLOCKS)]
-        inv_sum = [work.tile([P, 1], F32, name=f"inv_sum{i}") for i in range(QUERY_BLOCKS)]
-        for i in blocks:
+            weights = work.tile([P, N], BF16, name="weights")
+            row_sum = work.tile([P, 1], F32, name="row_sum")
             nc.scalar.activation(
-                weights[i][:], scores[i][:], ACT.Exp, bias=neg_max[i][:], scale=1.0, accum_out=row_sum[i][:]
+                weights[:, :keys], scores[:, :keys], ACT.Exp, bias=neg_max[:], scale=1.0, accum_out=row_sum[:]
             )
-        for i in blocks:
-            nc.vector.reciprocal(inv_sum[i][:], row_sum[i][:])
+            inv_sum = work.tile([P, 1], F32, name="inv_sum")
+            nc.vector.reciprocal(inv_sum[:], row_sum[:])
 
-        weights_flipped_ps = [psum.tile([P, keys[i]], BF16, name=f"weights_flipped_ps{i}") for i in range(QUERY_BLOCKS)]
-        weights_flipped = [work.tile([P, keys[i]], BF16, name=f"weights_flipped{i}") for i in range(QUERY_BLOCKS)]
-        for i in blocks:
+            weights_flipped_ps = psum.tile([P, N], BF16, name="weights_flipped_ps")
             for b in range(i + 1):
-                nc.tensor.transpose(weights_flipped_ps[i][:, rows[b]], weights[i][:, rows[b]], identity[:])
-        nc.vector.tensor_copy(weights_flipped[1][:], weights_flipped_ps[1][:])
-        nc.scalar.copy(weights_flipped[0][:], weights_flipped_ps[0][:])
+                nc.tensor.transpose(weights_flipped_ps[:, b * P : (b + 1) * P], weights[:, b * P : (b + 1) * P], identity[:])
+            weights_flipped = work.tile([P, N], BF16, name="weights_flipped")
+            nc.vector.tensor_copy(weights_flipped[:, :keys], weights_flipped_ps[:, :keys])
 
-        out_ps = [psum.tile([P, D], F32, name=f"out_ps{i}") for i in range(QUERY_BLOCKS)]
-        out_rows = [work.tile([P, D], F32, name=f"out_rows{i}") for i in range(QUERY_BLOCKS)]
-        for i in blocks:
+            out_ps = psum.tile([P, D], F32, name="out_ps")
             for b in range(i + 1):
-                nc.tensor.matmul(out_ps[i][:], weights_flipped[i][:, rows[b]], v_rows[:, b, :], start=(b == 0), stop=(b == i))
-        nc.vector.tensor_scalar_mul(out_rows[1][:], out_ps[1][:], inv_sum[1][:])
-        nc.sync.dma_start(out[rows[1], :], out_rows[1][:])
-        nc.scalar.mul(out_rows[0][:], out_ps[0][:], inv_sum[0][:])
-        nc.scalar.dma_start(out[rows[0], :], out_rows[0][:])
+                nc.tensor.matmul(
+                    out_ps[:], weights_flipped[:, b * P : (b + 1) * P], v_rows[:, b, :], start=(b == 0), stop=(b == i)
+                )
+            out_rows = work.tile([P, D], F32, name="out_rows")
+            nc.vector.tensor_scalar_mul(out_rows[:], out_ps[:], inv_sum[:])
+            nc.sync.dma_start(out[rows, :], out_rows[:])

@@ -45,20 +45,41 @@ def tile_pagedattention_kernel(tc, q, table, k_scale, v, offs, out):
         nc.vector.memset(identity[:], 0.0)
         make_identity(nc, identity[:], nomemset=True)
 
-        causal_bias = held.tile([P, P], F32, name="causal_bias")
-        nc.vector.memset(causal_bias[:], 0.0)
+        diagonal_bias = held.tile([P, P], F32, name="diagonal_bias")
+        nc.vector.memset(diagonal_bias[:], 0.0)
         nc.gpsimd.affine_select(
-            out=causal_bias[:],
-            in_=causal_bias[:],
+            out=diagonal_bias[:],
+            in_=diagonal_bias[:],
             pattern=[[-1, P]],
             compare_op=ALU.is_ge,
             fill=MASKED,
             base=0,
             channel_multiplier=1,
         )
+        causal_bias = held.tile([P, N], BF16, name="causal_bias")
+        nc.vector.memset(causal_bias[:, : N - P], 0.0)
+        nc.vector.tensor_copy(causal_bias[:, N - P :], diagonal_bias[:])
 
         key_scale = held.tile([P, N], F32, name="key_scale")
         nc.vector.tensor_scalar_mul(key_scale[:], key_scale_raw[:], 1.0 / math.sqrt(D))
+
+        keys = [(i + 1) * P for i in range(QUERY_BLOCKS)]
+
+        seen_scale = [held.tile([P, keys[i]], F32, name=f"seen_scale{i}") for i in range(QUERY_BLOCKS)]
+        for i in reversed(range(QUERY_BLOCKS)):
+            nc.gpsimd.affine_select(
+                out=seen_scale[i][:],
+                in_=key_scale[:, : keys[i]],
+                pattern=[[-1, keys[i]]],
+                compare_op=ALU.is_ge,
+                fill=1.0,
+                base=i * P,
+                channel_multiplier=1,
+            )
+
+        scores_ps = [psum.tile([P, keys[i]], F32, name="scores_ps") for i in range(QUERY_BLOCKS)]
+        for i in reversed(range(QUERY_BLOCKS)):
+            nc.tensor.matmul(scores_ps[i][:], identity[:], causal_bias[:, N - keys[i] :], start=True, stop=False)
 
         table_cols = held.tile([D, S], BF16, name="table_cols")
         for half in range(2):
@@ -68,37 +89,34 @@ def tile_pagedattention_kernel(tc, q, table, k_scale, v, offs, out):
             nc.vector.tensor_copy(table_cols[:, 2 * half * P : 2 * (half + 1) * P], flipped[:])
 
         for i in reversed(range(QUERY_BLOCKS)):
-            keys = (i + 1) * P
             rows = slice(i * P, (i + 1) * P)
 
-            scores_ps = psum.tile([P, N], F32, name="scores_ps")
             nc.tensor.matmul(
-                scores_ps[:, :keys],
+                scores_ps[i][:],
                 q_cols[:, rows],
-                table_cols[:].indirect(offsets[:, : keys // 16]),
-                start=True,
+                table_cols[:].indirect(offsets[:, : keys[i] // 16]),
+                start=False,
                 stop=True,
             )
 
-            scores = work.tile([P, N], F32, name="scores")
-            nc.vector.tensor_tensor(scores[:, :keys], scores_ps[:, :keys], key_scale[:, :keys], ALU.mult)
-            nc.vector.tensor_tensor(scores[:, rows], scores[:, rows], causal_bias[:], ALU.add)
+            scores = work.tile([P, keys[i]], F32, name="scores")
+            nc.vector.tensor_tensor(scores[:], scores_ps[i][:], seen_scale[i][:], ALU.mult)
             neg_max = work.tile([P, 1], F32, name="neg_max")
-            nc.vector.reduce_max(neg_max[:], scores[:, :keys], axis=mybir.AxisListType.X, negate=True)
+            nc.vector.reduce_max(neg_max[:], scores[:], axis=mybir.AxisListType.X, negate=True)
 
-            weights = work.tile([P, N], BF16, name="weights")
+            weights = work.tile([P, keys[i]], BF16, name="weights")
             row_sum = work.tile([P, 1], F32, name="row_sum")
             nc.scalar.activation(
-                weights[:, :keys], scores[:, :keys], ACT.Exp, bias=neg_max[:], scale=1.0, accum_out=row_sum[:]
+                weights[:], scores[:], ACT.Exp, bias=neg_max[:], scale=1.0, accum_out=row_sum[:]
             )
             inv_sum = work.tile([P, 1], F32, name="inv_sum")
             nc.vector.reciprocal(inv_sum[:], row_sum[:])
 
-            weights_flipped_ps = psum.tile([P, N], BF16, name="weights_flipped_ps")
+            weights_flipped_ps = psum.tile([P, keys[i]], BF16, name="weights_flipped_ps")
             for b in range(i + 1):
                 nc.tensor.transpose(weights_flipped_ps[:, b * P : (b + 1) * P], weights[:, b * P : (b + 1) * P], identity[:])
-            weights_flipped = work.tile([P, N], BF16, name="weights_flipped")
-            nc.vector.tensor_copy(weights_flipped[:, :keys], weights_flipped_ps[:, :keys])
+            weights_flipped = work.tile([P, keys[i]], BF16, name="weights_flipped")
+            nc.vector.tensor_copy(weights_flipped[:], weights_flipped_ps[:])
 
             out_ps = psum.tile([P, D], F32, name="out_ps")
             for b in range(i + 1):

@@ -31,8 +31,8 @@ def tile_pagedattention_kernel(tc, q, table, k_scale, v, offs, out):
         nc.sync.dma_start(offsets[:], offs)
         q_cols = held.tile([D, M], BF16, name="q_cols")
         nc.sync.dma_start(q_cols[:], q)
-        key_scale_raw = held.tile([P, N], F32, name="key_scale_raw")
-        nc.scalar.dma_start(key_scale_raw[:], k_scale.rearrange("o n -> (o n)").partition_broadcast(P))
+        key_scale = held.tile([P, N], F32, name="key_scale")
+        nc.scalar.dma_start(key_scale[:], k_scale.rearrange("o n -> (o n)").partition_broadcast(P))
         v_rows = held.tile([P, KEY_BLOCKS, D], BF16, name="v_rows")
         nc.sync.dma_start(v_rows[:], v.rearrange("(b p) e -> p b e", p=P))
 
@@ -59,9 +59,6 @@ def tile_pagedattention_kernel(tc, q, table, k_scale, v, offs, out):
         causal_bias = held.tile([P, N], BF16, name="causal_bias")
         nc.vector.memset(causal_bias[:, : N - P], 0.0)
         nc.vector.tensor_copy(causal_bias[:, N - P :], diagonal_bias[:])
-
-        key_scale = held.tile([P, N], F32, name="key_scale")
-        nc.vector.tensor_scalar_mul(key_scale[:], key_scale_raw[:], 1.0 / math.sqrt(D))
 
         keys = [(i + 1) * P for i in range(QUERY_BLOCKS)]
 
@@ -100,7 +97,14 @@ def tile_pagedattention_kernel(tc, q, table, k_scale, v, offs, out):
             )
 
             scores = work.tile([P, keys[i]], F32, name="scores")
-            nc.vector.tensor_tensor(scores[:], scores_ps[i][:], seen_scale[i][:], ALU.mult)
+            nc.vector.scalar_tensor_tensor(
+                out=scores[:],
+                in0=scores_ps[i][:],
+                scalar=1.0 / math.sqrt(D),
+                in1=seen_scale[i][:],
+                op0=ALU.mult,
+                op1=ALU.mult,
+            )
             neg_max = work.tile([P, 1], F32, name="neg_max")
             nc.vector.reduce_max(neg_max[:], scores[:], axis=mybir.AxisListType.X, negate=True)
 

@@ -85,33 +85,36 @@ def tile_pagedattention_kernel(tc, q, table, k_scale, v, offs, out):
                 nc.tensor.transpose(flipped[:, k * P : (k + 1) * P], table_rows[:, 2 * half + k, :], identity[:])
             nc.vector.tensor_copy(table_cols[:, 2 * half * P : 2 * (half + 1) * P], flipped[:])
 
-        for i in reversed(range(QUERY_BLOCKS)):
-            rows = slice(i * P, (i + 1) * P)
+        order = list(reversed(range(QUERY_BLOCKS)))
 
+        for i in order:
             nc.tensor.matmul(
                 scores_ps[i][:],
-                q_cols[:, rows],
+                q_cols[:, i * P : (i + 1) * P],
                 table_cols[:].indirect(offsets[:, : keys[i] // 16]),
                 start=False,
                 stop=True,
             )
 
-            scores = work.tile([P, keys[i]], F32, name="scores")
+        scores = [work.tile([P, keys[i]], F32, name="scores") for i in range(QUERY_BLOCKS)]
+        neg_max = [work.tile([P, 1], F32, name="neg_max") for i in range(QUERY_BLOCKS)]
+        for i in order:
             nc.vector.scalar_tensor_tensor(
-                out=scores[:],
+                out=scores[i][:],
                 in0=scores_ps[i][:],
                 scalar=1.0 / math.sqrt(D),
                 in1=seen_scale[i][:],
                 op0=ALU.mult,
                 op1=ALU.mult,
             )
-            neg_max = work.tile([P, 1], F32, name="neg_max")
-            nc.vector.reduce_max(neg_max[:], scores[:], axis=mybir.AxisListType.X, negate=True)
+        for i in order:
+            nc.vector.reduce_max(neg_max[i][:], scores[i][:], axis=mybir.AxisListType.X, negate=True)
 
+        for i in order:
             weights = work.tile([P, keys[i]], BF16, name="weights")
             row_sum = work.tile([P, 1], F32, name="row_sum")
             nc.scalar.activation(
-                weights[:], scores[:], ACT.Exp, bias=neg_max[:], scale=1.0, accum_out=row_sum[:]
+                weights[:], scores[i][:], ACT.Exp, bias=neg_max[i][:], scale=1.0, accum_out=row_sum[:]
             )
             inv_sum = work.tile([P, 1], F32, name="inv_sum")
             nc.vector.reciprocal(inv_sum[:], row_sum[:])
@@ -129,4 +132,4 @@ def tile_pagedattention_kernel(tc, q, table, k_scale, v, offs, out):
                 )
             out_rows = work.tile([P, D], F32, name="out_rows")
             nc.vector.tensor_scalar_mul(out_rows[:], out_ps[:], inv_sum[:])
-            nc.sync.dma_start(out[rows, :], out_rows[:])
+            nc.sync.dma_start(out[i * P : (i + 1) * P, :], out_rows[:])

@@ -7,6 +7,7 @@ S, D, M, N = 512, 128, 256, 256
 P = 128
 SLOT_BLOCKS, QUERY_BLOCKS, KEY_BLOCKS = S // P, M // P, N // P
 MASKED = -1.0e30
+LOWEST = -3.0e38
 
 FLOPS = 2 * 2 * D * (M * (M + 1) // 2)
 
@@ -31,8 +32,8 @@ def tile_pagedattention_kernel(tc, q, table, k_scale, v, offs, out):
         nc.sync.dma_start(offsets[:], offs)
         q_cols = held.tile([D, M], BF16, name="q_cols")
         nc.sync.dma_start(q_cols[:], q)
-        key_scale = held.tile([P, N], F32, name="key_scale")
-        nc.scalar.dma_start(key_scale[:], k_scale.rearrange("o n -> (o n)").partition_broadcast(P))
+        scale_cols = held.tile([P, P + N], F32, name="scale_cols")
+        nc.scalar.dma_start(scale_cols[:, P:], k_scale.rearrange("o n -> (o n)").partition_broadcast(P))
         v_rows = held.tile([P, KEY_BLOCKS, D], BF16, name="v_rows")
         nc.sync.dma_start(v_rows[:], v.rearrange("(b p) e -> p b e", p=P))
 
@@ -60,19 +61,19 @@ def tile_pagedattention_kernel(tc, q, table, k_scale, v, offs, out):
         nc.vector.memset(causal_bias[:, : N - P], 0.0)
         nc.vector.tensor_copy(causal_bias[:, N - P :], diagonal_bias[:])
 
-        keys = [(i + 1) * P for i in range(QUERY_BLOCKS)]
+        scale_floor = held.tile([P, P], F32, name="scale_floor")
+        nc.vector.memset(scale_floor[:], LOWEST)
+        nc.gpsimd.affine_select(
+            out=scale_floor[:],
+            in_=scale_floor[:],
+            pattern=[[-1, P]],
+            compare_op=ALU.is_ge,
+            fill=1.0,
+            base=0,
+            channel_multiplier=1,
+        )
 
-        seen_scale = [held.tile([P, keys[i]], F32, name=f"seen_scale{i}") for i in range(QUERY_BLOCKS)]
-        for i in reversed(range(QUERY_BLOCKS)):
-            nc.gpsimd.affine_select(
-                out=seen_scale[i][:],
-                in_=key_scale[:, : keys[i]],
-                pattern=[[-1, keys[i]]],
-                compare_op=ALU.is_ge,
-                fill=1.0,
-                base=i * P,
-                channel_multiplier=1,
-            )
+        keys = [(i + 1) * P for i in range(QUERY_BLOCKS)]
 
         scores_ps = [psum.tile([P, keys[i]], F32, name="scores_ps") for i in range(QUERY_BLOCKS)]
         for i in reversed(range(QUERY_BLOCKS)):
@@ -84,6 +85,10 @@ def tile_pagedattention_kernel(tc, q, table, k_scale, v, offs, out):
             for k in range(2):
                 nc.tensor.transpose(flipped[:, k * P : (k + 1) * P], table_rows[:, 2 * half + k, :], identity[:])
             nc.vector.tensor_copy(table_cols[:, 2 * half * P : 2 * (half + 1) * P], flipped[:])
+
+        nc.vector.tensor_tensor(out=scale_cols[:, :P], in0=scale_cols[:, P : 2 * P], in1=scale_floor[:], op=ALU.max)
+        nc.vector.tensor_tensor(out=scale_cols[:, 2 * P :], in0=scale_cols[:, 2 * P :], in1=scale_floor[:], op=ALU.max)
+        seen_scale = [scale_cols[:, :P], scale_cols[:, P:]]
 
         order = list(reversed(range(QUERY_BLOCKS)))
 
@@ -103,7 +108,7 @@ def tile_pagedattention_kernel(tc, q, table, k_scale, v, offs, out):
                 out=scores[i][:],
                 in0=scores_ps[i][:],
                 scalar=1.0 / math.sqrt(D),
-                in1=seen_scale[i][:],
+                in1=seen_scale[i],
                 op0=ALU.mult,
                 op1=ALU.mult,
             )

@@ -1,13 +1,13 @@
 import math
 
 import concourse.mybir as mybir
-from concourse.masks import make_identity
 
 S, D, M, N = 512, 128, 256, 256
 P = 128
 SLOT_BLOCKS, QUERY_BLOCKS, KEY_BLOCKS = S // P, M // P, N // P
 MASKED = -1.0e30
-LOWEST = -3.0e38
+STEEP = 1.0e36
+QUADRANT = 32
 
 FLOPS = 2 * 2 * D * (M * (M + 1) // 2)
 
@@ -42,35 +42,36 @@ def tile_pagedattention_kernel(tc, q, table, k_scale, v, offs, out):
         nc.vector.memset(warm[:], 0.0)
         nc.scalar.activation(warmed[:], warm[:], ACT.Exp)
 
-        identity = held.tile([P, P], BF16, name="identity")
-        nc.vector.memset(identity[:], 0.0)
-        make_identity(nc, identity[:], nomemset=True)
-
-        diagonal_bias = held.tile([P, P], F32, name="diagonal_bias")
-        nc.vector.memset(diagonal_bias[:], 0.0)
-        nc.gpsimd.affine_select(
-            out=diagonal_bias[:],
-            in_=diagonal_bias[:],
-            pattern=[[-1, P]],
-            compare_op=ALU.is_ge,
-            fill=MASKED,
-            base=0,
-            channel_multiplier=1,
+        quadrant_base = held.tile([P, 1], F32, name="quadrant_base")
+        for first in range(0, P, QUADRANT):
+            nc.vector.memset(quadrant_base[first : first + QUADRANT, :], float(first))
+        ones = held.tile([P, P], F32, name="ones")
+        nc.vector.memset(ones[:], 1.0)
+        counted = held.tile([P, P], F32, name="counted", align_bytes=64)
+        nc.vector.tensor_tensor_scan(
+            out=counted[:], data0=ones[:], data1=ones[:], initial=quadrant_base[:], op0=ALU.mult, op1=ALU.add
         )
+        turned = held.tile([P, QUADRANT], F32, name="turned", align_bytes=64)
+        nc.vector.transpose(turned[:], counted[:, :QUADRANT])
+        diagonal = held.tile([P, 1], F32, name="diagonal")
+        nc.vector.tensor_scalar(
+            out=diagonal[:], in0=turned[:, 0:1], scalar1=quadrant_base[:], scalar2=0.5, op0=ALU.add, op1=ALU.add
+        )
+
+        identity = held.tile([P, P], BF16, name="identity")
+        nc.vector.tensor_scalar(
+            out=identity[:], in0=counted[:], scalar1=diagonal[:], scalar2=-0.5, op0=ALU.subtract, op1=ALU.is_equal
+        )
+
         causal_bias = held.tile([P, N], BF16, name="causal_bias")
         nc.vector.memset(causal_bias[:, : N - P], 0.0)
-        nc.vector.tensor_copy(causal_bias[:, N - P :], diagonal_bias[:])
+        nc.vector.tensor_scalar(
+            out=causal_bias[:, N - P :], in0=counted[:], scalar1=diagonal[:], scalar2=MASKED, op0=ALU.is_gt, op1=ALU.mult
+        )
 
-        scale_floor = held.tile([P, P], F32, name="scale_floor")
-        nc.vector.memset(scale_floor[:], LOWEST)
-        nc.gpsimd.affine_select(
-            out=scale_floor[:],
-            in_=scale_floor[:],
-            pattern=[[-1, P]],
-            compare_op=ALU.is_ge,
-            fill=1.0,
-            base=0,
-            channel_multiplier=1,
+        steep = held.tile([P, P], F32, name="steep")
+        nc.vector.tensor_scalar(
+            out=steep[:], in0=counted[:], scalar1=diagonal[:], scalar2=STEEP, op0=ALU.subtract, op1=ALU.mult
         )
 
         keys = [(i + 1) * P for i in range(QUERY_BLOCKS)]
@@ -86,8 +87,12 @@ def tile_pagedattention_kernel(tc, q, table, k_scale, v, offs, out):
                 nc.tensor.transpose(flipped[:, k * P : (k + 1) * P], table_rows[:, 2 * half + k, :], identity[:])
             nc.vector.tensor_copy(table_cols[:, 2 * half * P : 2 * (half + 1) * P], flipped[:])
 
-        nc.vector.tensor_tensor(out=scale_cols[:, :P], in0=scale_cols[:, P : 2 * P], in1=scale_floor[:], op=ALU.max)
-        nc.vector.tensor_tensor(out=scale_cols[:, 2 * P :], in0=scale_cols[:, 2 * P :], in1=scale_floor[:], op=ALU.max)
+        nc.vector.scalar_tensor_tensor(
+            out=scale_cols[:, :P], in0=steep[:], scalar=1.0, in1=scale_cols[:, P : 2 * P], op0=ALU.min, op1=ALU.max
+        )
+        nc.vector.scalar_tensor_tensor(
+            out=scale_cols[:, 2 * P :], in0=steep[:], scalar=1.0, in1=scale_cols[:, 2 * P :], op0=ALU.min, op1=ALU.max
+        )
         seen_scale = [scale_cols[:, :P], scale_cols[:, P:]]
 
         order = list(reversed(range(QUERY_BLOCKS)))

@@ -37,48 +37,47 @@ def tile_pagedattention_kernel(tc, q, table, k_scale, v, offs, out):
         v_rows = held.tile([P, KEY_BLOCKS, D], BF16, name="v_rows")
         nc.sync.dma_start(v_rows[:], v.rearrange("(b p) e -> p b e", p=P))
 
-        warm = held.tile([P, 1], F32, name="warm")
+        one = held.tile([P, 1], F32, name="one")
+        nc.vector.memset(one[:], 1.0)
+        counted = held.tile([P, P], F32, name="counted", align_bytes=64)
+        nc.vector.tensor_tensor_scan(
+            out=counted[:],
+            data0=one[:].to_broadcast([P, P]),
+            data1=one[:].to_broadcast([P, P]),
+            initial=0.0,
+            op0=ALU.mult,
+            op1=ALU.add,
+        )
+        turned = held.tile([P, QUADRANT], F32, name="turned", align_bytes=64)
+        nc.vector.transpose(turned[:], counted[:, :QUADRANT])
+        own = turned[:, 0:1]
+
         warmed = held.tile([P, 1], F32, name="warmed")
-        nc.vector.memset(warm[:], 0.0)
-        nc.scalar.activation(warmed[:], warm[:], ACT.Exp)
+        nc.scalar.activation(warmed[:], one[:], ACT.Exp)
 
         quadrant_base = held.tile([P, 1], F32, name="quadrant_base")
         for first in range(0, P, QUADRANT):
             nc.vector.memset(quadrant_base[first : first + QUADRANT, :], float(first))
-        ones = held.tile([P, P], F32, name="ones")
-        nc.vector.memset(ones[:], 1.0)
-        counted = held.tile([P, P], F32, name="counted", align_bytes=64)
-        nc.vector.tensor_tensor_scan(
-            out=counted[:], data0=ones[:], data1=ones[:], initial=quadrant_base[:], op0=ALU.mult, op1=ALU.add
-        )
-        turned = held.tile([P, QUADRANT], F32, name="turned", align_bytes=64)
-        nc.vector.transpose(turned[:], counted[:, :QUADRANT])
-        diagonal = held.tile([P, 1], F32, name="diagonal")
-        nc.vector.tensor_scalar(
-            out=diagonal[:], in0=turned[:, 0:1], scalar1=quadrant_base[:], scalar2=0.5, op0=ALU.add, op1=ALU.add
-        )
+        local = held.tile([P, P], F32, name="local")
+        nc.vector.tensor_scalar(out=local[:], in0=counted[:], scalar1=quadrant_base[:], scalar2=None, op0=ALU.subtract)
 
         identity = held.tile([P, P], BF16, name="identity")
-        nc.vector.tensor_scalar(
-            out=identity[:], in0=counted[:], scalar1=diagonal[:], scalar2=-0.5, op0=ALU.subtract, op1=ALU.is_equal
-        )
+        nc.vector.tensor_scalar(out=identity[:], in0=local[:], scalar1=own, scalar2=None, op0=ALU.is_equal)
 
         causal_bias = held.tile([P, N], BF16, name="causal_bias")
         nc.vector.memset(causal_bias[:, : N - P], 0.0)
         nc.vector.tensor_scalar(
-            out=causal_bias[:, N - P :], in0=counted[:], scalar1=diagonal[:], scalar2=MASKED, op0=ALU.is_gt, op1=ALU.mult
+            out=causal_bias[:, N - P :], in0=local[:], scalar1=own, scalar2=MASKED, op0=ALU.is_gt, op1=ALU.mult
         )
 
+        own_and_half = held.tile([P, 1], F32, name="own_and_half")
+        nc.vector.tensor_scalar_add(own_and_half[:], own, 0.5)
         steep = held.tile([P, P], F32, name="steep")
         nc.vector.tensor_scalar(
-            out=steep[:], in0=counted[:], scalar1=diagonal[:], scalar2=STEEP, op0=ALU.subtract, op1=ALU.mult
+            out=steep[:], in0=local[:], scalar1=own_and_half[:], scalar2=STEEP, op0=ALU.subtract, op1=ALU.mult
         )
 
         keys = [(i + 1) * P for i in range(QUERY_BLOCKS)]
-
-        scores_ps = [psum.tile([P, keys[i]], F32, name="scores_ps") for i in range(QUERY_BLOCKS)]
-        for i in reversed(range(QUERY_BLOCKS)):
-            nc.tensor.matmul(scores_ps[i][:], identity[:], causal_bias[:, N - keys[i] :], start=True, stop=False)
 
         table_cols = held.tile([D, S], BF16, name="table_cols")
         for half in range(2):
@@ -86,6 +85,10 @@ def tile_pagedattention_kernel(tc, q, table, k_scale, v, offs, out):
             for k in range(2):
                 nc.tensor.transpose(flipped[:, k * P : (k + 1) * P], table_rows[:, 2 * half + k, :], identity[:])
             nc.vector.tensor_copy(table_cols[:, 2 * half * P : 2 * (half + 1) * P], flipped[:])
+
+        scores_ps = [psum.tile([P, keys[i]], F32, name="scores_ps") for i in range(QUERY_BLOCKS)]
+        for i in reversed(range(QUERY_BLOCKS)):
+            nc.tensor.matmul(scores_ps[i][:], identity[:], causal_bias[:, N - keys[i] :], start=True, stop=False)
 
         nc.vector.scalar_tensor_tensor(
             out=scale_cols[:, :P], in0=steep[:], scalar=1.0, in1=scale_cols[:, P : 2 * P], op0=ALU.min, op1=ALU.max

@@ -21,7 +21,7 @@ def tile_pagedattention_kernel(tc, q, table, k_scale, v, offs, out):
     with (
         tc.tile_pool(name="held", bufs=1) as held,
         tc.tile_pool(name="work", bufs=2) as work,
-        tc.psum_pool(name="psum", bufs=2) as psum,
+        tc.psum_pool(name="score_psum", bufs=QUERY_BLOCKS) as score_psum,
     ):
         table_rows = held.tile([P, SLOT_BLOCKS, D], BF16, name="table_rows")
         table_blocks = table.rearrange("(b p) d -> p b d", p=P)
@@ -80,13 +80,13 @@ def tile_pagedattention_kernel(tc, q, table, k_scale, v, offs, out):
         keys = [(i + 1) * P for i in range(QUERY_BLOCKS)]
 
         table_cols = held.tile([D, S], BF16, name="table_cols")
-        for half in range(2):
-            flipped = psum.tile([D, 2 * P], BF16, name="flipped")
-            for k in range(2):
-                nc.tensor.transpose(flipped[:, k * P : (k + 1) * P], table_rows[:, 2 * half + k, :], identity[:])
-            nc.vector.tensor_copy(table_cols[:, 2 * half * P : 2 * (half + 1) * P], flipped[:])
+        with tc.psum_pool(name="flip_psum", bufs=SLOT_BLOCKS) as flip_psum:
+            for b in range(SLOT_BLOCKS):
+                flipped = flip_psum.tile([D, P], BF16, name="flipped")
+                nc.tensor.transpose(flipped[:], table_rows[:, b, :], identity[:])
+                nc.vector.tensor_copy(table_cols[:, b * P : (b + 1) * P], flipped[:])
 
-        scores_ps = [psum.tile([P, keys[i]], F32, name="scores_ps") for i in range(QUERY_BLOCKS)]
+        scores_ps = [score_psum.tile([P, keys[i]], F32, name="scores_ps") for i in range(QUERY_BLOCKS)]
         for i in reversed(range(QUERY_BLOCKS)):
             nc.tensor.matmul(scores_ps[i][:], identity[:], causal_bias[:, N - keys[i] :], start=True, stop=False)
 
@@ -123,26 +123,30 @@ def tile_pagedattention_kernel(tc, q, table, k_scale, v, offs, out):
         for i in order:
             nc.vector.reduce_max(neg_max[i][:], scores[i][:], axis=mybir.AxisListType.X, negate=True)
 
-        for i in order:
-            weights = work.tile([P, keys[i]], BF16, name="weights")
-            row_sum = work.tile([P, 1], F32, name="row_sum")
-            nc.scalar.activation(
-                weights[:], scores[i][:], ACT.Exp, bias=neg_max[i][:], scale=1.0, accum_out=row_sum[:]
-            )
-            inv_sum = work.tile([P, 1], F32, name="inv_sum")
-            nc.vector.reciprocal(inv_sum[:], row_sum[:])
-
-            weights_flipped_ps = psum.tile([P, keys[i]], BF16, name="weights_flipped_ps")
-            for b in range(i + 1):
-                nc.tensor.transpose(weights_flipped_ps[:, b * P : (b + 1) * P], weights[:, b * P : (b + 1) * P], identity[:])
-            weights_flipped = work.tile([P, keys[i]], BF16, name="weights_flipped")
-            nc.vector.tensor_copy(weights_flipped[:], weights_flipped_ps[:])
-
-            out_ps = psum.tile([P, D], F32, name="out_ps")
-            for b in range(i + 1):
-                nc.tensor.matmul(
-                    out_ps[:], weights_flipped[:, b * P : (b + 1) * P], v_rows[:, b, :], start=(b == 0), stop=(b == i)
+        with (
+            tc.psum_pool(name="flipped_psum", bufs=sum(keys) // P) as flipped_psum,
+            tc.psum_pool(name="psum", bufs=QUERY_BLOCKS) as psum,
+        ):
+            for i in order:
+                weights = work.tile([P, keys[i]], BF16, name="weights")
+                row_sum = work.tile([P, 1], F32, name="row_sum")
+                nc.scalar.activation(
+                    weights[:], scores[i][:], ACT.Exp, bias=neg_max[i][:], scale=1.0, accum_out=row_sum[:]
                 )
-            out_rows = work.tile([P, D], F32, name="out_rows")
-            nc.vector.tensor_scalar_mul(out_rows[:], out_ps[:], inv_sum[:])
-            nc.sync.dma_start(out[i * P : (i + 1) * P, :], out_rows[:])
+                inv_sum = work.tile([P, 1], F32, name="inv_sum")
+                nc.vector.reciprocal(inv_sum[:], row_sum[:])
+
+                weights_flipped = work.tile([P, keys[i]], BF16, name="weights_flipped")
+                for b in range(i + 1):
+                    weights_flipped_ps = flipped_psum.tile([P, P], BF16, name="weights_flipped_ps")
+                    nc.tensor.transpose(weights_flipped_ps[:], weights[:, b * P : (b + 1) * P], identity[:])
+                    nc.vector.tensor_copy(weights_flipped[:, b * P : (b + 1) * P], weights_flipped_ps[:])
+
+                out_ps = psum.tile([P, D], F32, name="out_ps")
+                for b in range(i + 1):
+                    nc.tensor.matmul(
+                        out_ps[:], weights_flipped[:, b * P : (b + 1) * P], v_rows[:, b, :], start=(b == 0), stop=(b == i)
+                    )
+                out_rows = work.tile([P, D], F32, name="out_rows")
+                nc.vector.tensor_scalar_mul(out_rows[:], out_ps[:], inv_sum[:])
+                nc.sync.dma_start(out[i * P : (i + 1) * P, :], out_rows[:])

@@ -5,6 +5,7 @@ import concourse.mybir as mybir
 S, D, M, N = 512, 128, 256, 256
 P = 128
 SLOT_BLOCKS, QUERY_BLOCKS, KEY_BLOCKS = S // P, M // P, N // P
+SCORE_TILES = QUERY_BLOCKS * (QUERY_BLOCKS + 1) // 2
 MASKED = -1.0e30
 STEEP = 1.0e36
 QUADRANT = 32
@@ -21,7 +22,7 @@ def tile_pagedattention_kernel(tc, q, table, k_scale, v, offs, out):
     with (
         tc.tile_pool(name="held", bufs=1) as held,
         tc.tile_pool(name="work", bufs=2) as work,
-        tc.psum_pool(name="score_psum", bufs=QUERY_BLOCKS) as score_psum,
+        tc.psum_pool(name="score_psum", bufs=SCORE_TILES) as score_psum,
     ):
         table_rows = held.tile([P, SLOT_BLOCKS, D], BF16, name="table_rows")
         table_blocks = table.rearrange("(b p) d -> p b d", p=P)
@@ -32,8 +33,8 @@ def tile_pagedattention_kernel(tc, q, table, k_scale, v, offs, out):
         nc.sync.dma_start(offsets[:], offs)
         q_cols = held.tile([D, M], BF16, name="q_cols")
         nc.sync.dma_start(q_cols[:], q)
-        scale_cols = held.tile([P, P + N], F32, name="scale_cols")
-        nc.scalar.dma_start(scale_cols[:, P:], k_scale.rearrange("o n -> (o n)").partition_broadcast(P))
+        key_scale = held.tile([P, N], F32, name="key_scale")
+        nc.scalar.dma_start(key_scale[:], k_scale.rearrange("o n -> (o n)").partition_broadcast(P))
         v_rows = held.tile([P, KEY_BLOCKS, D], BF16, name="v_rows")
         nc.sync.dma_start(v_rows[:], v.rearrange("(b p) e -> p b e", p=P))
 
@@ -64,10 +65,9 @@ def tile_pagedattention_kernel(tc, q, table, k_scale, v, offs, out):
         identity = held.tile([P, P], BF16, name="identity")
         nc.vector.tensor_scalar(out=identity[:], in0=local[:], scalar1=own, scalar2=None, op0=ALU.is_equal)
 
-        causal_bias = held.tile([P, N], BF16, name="causal_bias")
-        nc.vector.memset(causal_bias[:, : N - P], 0.0)
+        causal_bias = held.tile([P, P], BF16, name="causal_bias")
         nc.vector.tensor_scalar(
-            out=causal_bias[:, N - P :], in0=local[:], scalar1=own, scalar2=MASKED, op0=ALU.is_gt, op1=ALU.mult
+            out=causal_bias[:], in0=local[:], scalar1=own, scalar2=MASKED, op0=ALU.is_gt, op1=ALU.mult
         )
 
         own_and_half = held.tile([P, 1], F32, name="own_and_half")
@@ -78,6 +78,8 @@ def tile_pagedattention_kernel(tc, q, table, k_scale, v, offs, out):
         )
 
         keys = [(i + 1) * P for i in range(QUERY_BLOCKS)]
+        order = list(reversed(range(QUERY_BLOCKS)))
+        tiles = [(i, b) for i in order for b in range(i + 1)]
 
         table_cols = held.tile([D, S], BF16, name="table_cols")
         with tc.psum_pool(name="flip_psum", bufs=SLOT_BLOCKS) as flip_psum:
@@ -86,37 +88,38 @@ def tile_pagedattention_kernel(tc, q, table, k_scale, v, offs, out):
                 nc.tensor.transpose(flipped[:], table_rows[:, b, :], identity[:])
                 nc.vector.tensor_copy(table_cols[:, b * P : (b + 1) * P], flipped[:])
 
-        scores_ps = [score_psum.tile([P, keys[i]], F32, name="scores_ps") for i in range(QUERY_BLOCKS)]
-        for i in reversed(range(QUERY_BLOCKS)):
-            nc.tensor.matmul(scores_ps[i][:], identity[:], causal_bias[:, N - keys[i] :], start=True, stop=False)
-
-        nc.vector.scalar_tensor_tensor(
-            out=scale_cols[:, :P], in0=steep[:], scalar=1.0, in1=scale_cols[:, P : 2 * P], op0=ALU.min, op1=ALU.max
-        )
-        nc.vector.scalar_tensor_tensor(
-            out=scale_cols[:, 2 * P :], in0=steep[:], scalar=1.0, in1=scale_cols[:, 2 * P :], op0=ALU.min, op1=ALU.max
-        )
-        seen_scale = [scale_cols[:, :P], scale_cols[:, P:]]
-
-        order = list(reversed(range(QUERY_BLOCKS)))
-
+        scores_ps = {pair: score_psum.tile([P, P], F32, name="scores_ps") for pair in tiles}
         for i in order:
+            nc.tensor.matmul(scores_ps[(i, i)][:], identity[:], causal_bias[:], start=True, stop=False)
+
+        seen_scale = held.tile([P, N], F32, name="seen_scale")
+        nc.vector.scalar_tensor_tensor(
+            out=seen_scale[:].rearrange("p (b j) -> p b j", j=P),
+            in0=steep[:].unsqueeze(1).to_broadcast([P, KEY_BLOCKS, P]),
+            scalar=1.0,
+            in1=key_scale[:].rearrange("p (b j) -> p b j", j=P),
+            op0=ALU.min,
+            op1=ALU.max,
+        )
+
+        for i, b in tiles:
             nc.tensor.matmul(
-                scores_ps[i][:],
+                scores_ps[(i, b)][:],
                 q_cols[:, i * P : (i + 1) * P],
-                table_cols[:].indirect(offsets[:, : keys[i] // 16]),
-                start=False,
+                table_cols[:].indirect(offsets[:, b * P // 16 : (b + 1) * P // 16]),
+                start=(b != i),
                 stop=True,
             )
 
         scores = [work.tile([P, keys[i]], F32, name="scores") for i in range(QUERY_BLOCKS)]
         neg_max = [work.tile([P, 1], F32, name="neg_max") for i in range(QUERY_BLOCKS)]
-        for i in order:
+        for i, b in tiles:
+            tile_scale = seen_scale if b == i else key_scale
             nc.vector.scalar_tensor_tensor(
-                out=scores[i][:],
-                in0=scores_ps[i][:],
+                out=scores[i][:, b * P : (b + 1) * P],
+                in0=scores_ps[(i, b)][:],
                 scalar=1.0 / math.sqrt(D),
-                in1=seen_scale[i],
+                in1=tile_scale[:, b * P : (b + 1) * P],
                 op0=ALU.mult,
                 op1=ALU.mult,
             )
@@ -124,7 +127,7 @@ def tile_pagedattention_kernel(tc, q, table, k_scale, v, offs, out):
             nc.vector.reduce_max(neg_max[i][:], scores[i][:], axis=mybir.AxisListType.X, negate=True)
 
         with (
-            tc.psum_pool(name="flipped_psum", bufs=sum(keys) // P) as flipped_psum,
+            tc.psum_pool(name="flipped_psum", bufs=SCORE_TILES) as flipped_psum,
             tc.psum_pool(name="psum", bufs=QUERY_BLOCKS) as psum,
         ):
             for i in order:

@@ -7,8 +7,6 @@ P = 128
 SLOT_BLOCKS, QUERY_BLOCKS, KEY_BLOCKS = S // P, M // P, N // P
 SCORE_TILES = QUERY_BLOCKS * (QUERY_BLOCKS + 1) // 2
 MASKED = -1.0e30
-STEEP = 1.0e36
-QUADRANT = 32
 
 FLOPS = 2 * 2 * D * (M * (M + 1) // 2)
 
@@ -38,48 +36,44 @@ def tile_pagedattention_kernel(tc, q, table, k_scale, v, offs, out):
         v_rows = held.tile([P, KEY_BLOCKS, D], BF16, name="v_rows")
         nc.sync.dma_start(v_rows[:], v.rearrange("(b p) e -> p b e", p=P))
 
-        one = held.tile([P, 1], F32, name="one")
-        nc.vector.memset(one[:], 1.0)
-        counted = held.tile([P, P], F32, name="counted", align_bytes=64)
-        nc.vector.tensor_tensor_scan(
-            out=counted[:],
-            data0=one[:].to_broadcast([P, P]),
-            data1=one[:].to_broadcast([P, P]),
-            initial=0.0,
-            op0=ALU.mult,
-            op1=ALU.add,
+        ahead = held.tile([P, P], F32, name="ahead")
+        nc.gpsimd.iota(
+            ahead[:], pattern=[[1, P]], base=0, channel_multiplier=-1, allow_small_or_imprecise_dtypes=True
         )
-        turned = held.tile([P, QUADRANT], F32, name="turned", align_bytes=64)
-        nc.vector.transpose(turned[:], counted[:, :QUADRANT])
-        own = turned[:, 0:1]
 
         warmed = held.tile([P, 1], F32, name="warmed")
-        nc.scalar.activation(warmed[:], one[:], ACT.Exp)
+        nc.vector.memset(warmed[:], 0.0)
+        nc.scalar.activation(warmed[:], warmed[:], ACT.Exp)
 
-        quadrant_base = held.tile([P, 1], F32, name="quadrant_base")
-        for first in range(0, P, QUADRANT):
-            nc.vector.memset(quadrant_base[first : first + QUADRANT, :], float(first))
-        local = held.tile([P, P], F32, name="local")
-        nc.vector.tensor_scalar(out=local[:], in0=counted[:], scalar1=quadrant_base[:], scalar2=None, op0=ALU.subtract)
+        identity_f32 = held.tile([P, P], F32, name="identity_f32")
+        nc.vector.tensor_scalar(out=identity_f32[:], in0=ahead[:], scalar1=0.0, scalar2=None, op0=ALU.is_equal)
 
-        identity = held.tile([P, P], BF16, name="identity")
-        nc.vector.tensor_scalar(out=identity[:], in0=local[:], scalar1=own, scalar2=None, op0=ALU.is_equal)
-
-        causal_bias = held.tile([P, P], BF16, name="causal_bias")
+        causal_bias = held.tile([P, P], F32, name="causal_bias")
         nc.vector.tensor_scalar(
-            out=causal_bias[:], in0=local[:], scalar1=own, scalar2=MASKED, op0=ALU.is_gt, op1=ALU.mult
+            out=causal_bias[:], in0=ahead[:], scalar1=0.0, scalar2=MASKED, op0=ALU.is_gt, op1=ALU.mult
         )
 
-        own_and_half = held.tile([P, 1], F32, name="own_and_half")
-        nc.vector.tensor_scalar_add(own_and_half[:], own, 0.5)
-        steep = held.tile([P, P], F32, name="steep")
-        nc.vector.tensor_scalar(
-            out=steep[:], in0=local[:], scalar1=own_and_half[:], scalar2=STEEP, op0=ALU.subtract, op1=ALU.mult
+        identity = held.tile([P, P], BF16, name="identity")
+        nc.vector.tensor_scalar(out=identity[:], in0=ahead[:], scalar1=0.0, scalar2=None, op0=ALU.is_equal)
+
+        seen_scale = held.tile([P, N], F32, name="seen_scale")
+        nc.gpsimd.affine_select(
+            out=seen_scale[:].rearrange("p (b j) -> p b j", j=P),
+            in_=key_scale[:].rearrange("p (b j) -> p b j", j=P),
+            pattern=[[0, KEY_BLOCKS], [-1, P]],
+            compare_op=ALU.is_ge,
+            fill=1.0,
+            base=0,
+            channel_multiplier=1,
         )
 
         keys = [(i + 1) * P for i in range(QUERY_BLOCKS)]
         order = list(reversed(range(QUERY_BLOCKS)))
         tiles = [(i, b) for i in order for b in range(i + 1)]
+
+        scores_ps = {pair: score_psum.tile([P, P], F32, name="scores_ps") for pair in tiles}
+        for i in order:
+            nc.tensor.matmul(scores_ps[(i, i)][:], identity_f32[:], causal_bias[:], start=True, stop=False)
 
         table_cols = held.tile([D, S], BF16, name="table_cols")
         with tc.psum_pool(name="flip_psum", bufs=SLOT_BLOCKS) as flip_psum:
@@ -87,20 +81,6 @@ def tile_pagedattention_kernel(tc, q, table, k_scale, v, offs, out):
                 flipped = flip_psum.tile([D, P], BF16, name="flipped")
                 nc.tensor.transpose(flipped[:], table_rows[:, b, :], identity[:])
                 nc.vector.tensor_copy(table_cols[:, b * P : (b + 1) * P], flipped[:])
-
-        scores_ps = {pair: score_psum.tile([P, P], F32, name="scores_ps") for pair in tiles}
-        for i in order:
-            nc.tensor.matmul(scores_ps[(i, i)][:], identity[:], causal_bias[:], start=True, stop=False)
-
-        seen_scale = held.tile([P, N], F32, name="seen_scale")
-        nc.vector.scalar_tensor_tensor(
-            out=seen_scale[:].rearrange("p (b j) -> p b j", j=P),
-            in0=steep[:].unsqueeze(1).to_broadcast([P, KEY_BLOCKS, P]),
-            scalar=1.0,
-            in1=key_scale[:].rearrange("p (b j) -> p b j", j=P),
-            op0=ALU.min,
-            op1=ALU.max,
-        )
 
         for i, b in tiles:
             nc.tensor.matmul(

@@ -7,6 +7,7 @@ P = 128
 SLOT_BLOCKS, QUERY_BLOCKS, KEY_BLOCKS = S // P, M // P, N // P
 SCORE_TILES = QUERY_BLOCKS * (QUERY_BLOCKS + 1) // 2
 MASKED = -1.0e30
+STEEP = 1.0e36
 
 FLOPS = 2 * 2 * D * (M * (M + 1) // 2)
 
@@ -20,9 +21,10 @@ def tile_pagedattention_kernel(tc, q, table, k_scale, v, offs, out):
     with (
         tc.tile_pool(name="held", bufs=1) as held,
         tc.tile_pool(name="work", bufs=2) as work,
+        tc.tile_pool(name="shared", bufs=1) as shared,
         tc.psum_pool(name="score_psum", bufs=SCORE_TILES) as score_psum,
     ):
-        table_rows = held.tile([P, SLOT_BLOCKS, D], BF16, name="table_rows")
+        table_rows = shared.tile([P, SLOT_BLOCKS, D], BF16, name="table_rows", tag="pool_then_scale")
         table_blocks = table.rearrange("(b p) d -> p b d", p=P)
         nc.sync.dma_start(table_rows[:, 0:2, :], table_blocks[:, 0:2, :])
         nc.scalar.dma_start(table_rows[:, 2:4, :], table_blocks[:, 2:4, :])
@@ -56,15 +58,9 @@ def tile_pagedattention_kernel(tc, q, table, k_scale, v, offs, out):
         identity = held.tile([P, P], BF16, name="identity")
         nc.vector.tensor_scalar(out=identity[:], in0=ahead[:], scalar1=0.0, scalar2=None, op0=ALU.is_equal)
 
-        seen_scale = held.tile([P, N], F32, name="seen_scale")
-        nc.gpsimd.affine_select(
-            out=seen_scale[:].rearrange("p (b j) -> p b j", j=P),
-            in_=key_scale[:].rearrange("p (b j) -> p b j", j=P),
-            pattern=[[0, KEY_BLOCKS], [-1, P]],
-            compare_op=ALU.is_ge,
-            fill=1.0,
-            base=0,
-            channel_multiplier=1,
+        steep = held.tile([P, P], F32, name="steep")
+        nc.vector.tensor_scalar(
+            out=steep[:], in0=ahead[:], scalar1=0.5, scalar2=STEEP, op0=ALU.subtract, op1=ALU.mult
         )
 
         keys = [(i + 1) * P for i in range(QUERY_BLOCKS)]
@@ -81,6 +77,16 @@ def tile_pagedattention_kernel(tc, q, table, k_scale, v, offs, out):
                 flipped = flip_psum.tile([D, P], BF16, name="flipped")
                 nc.tensor.transpose(flipped[:], table_rows[:, b, :], identity[:])
                 nc.vector.tensor_copy(table_cols[:, b * P : (b + 1) * P], flipped[:])
+
+        seen_scale = shared.tile([P, N], F32, name="seen_scale", tag="pool_then_scale")
+        nc.vector.scalar_tensor_tensor(
+            out=seen_scale[:].rearrange("p (b j) -> p b j", j=P),
+            in0=steep[:].unsqueeze(1).to_broadcast([P, KEY_BLOCKS, P]),
+            scalar=1.0,
+            in1=key_scale[:].rearrange("p (b j) -> p b j", j=P),
+            op0=ALU.min,
+            op1=ALU.max,
+        )
 
         for i, b in tiles:
             nc.tensor.matmul(

import math

import concourse.mybir as mybir

S, D, M, N = 512, 128, 256, 256
P = 128
SLOT_BLOCKS, QUERY_BLOCKS, KEY_BLOCKS = S // P, M // P, N // P
SCORE_TILES = QUERY_BLOCKS * (QUERY_BLOCKS + 1) // 2
MASKED = -1.0e30
STEEP = 1.0e36

FLOPS = 2 * 2 * D * (M * (M + 1) // 2)

BF16, F32, U16 = mybir.dt.bfloat16, mybir.dt.float32, mybir.dt.uint16
ALU = mybir.AluOpType
ACT = mybir.ActivationFunctionType


def tile_pagedattention_kernel(tc, q, table, k_scale, v, offs, out):
    nc = tc.nc
    with (
        tc.tile_pool(name="held", bufs=1) as held,
        tc.tile_pool(name="work", bufs=2) as work,
        tc.tile_pool(name="shared", bufs=1) as shared,
        tc.psum_pool(name="score_psum", bufs=SCORE_TILES) as score_psum,
    ):
        table_rows = shared.tile([P, SLOT_BLOCKS, D], BF16, name="table_rows", tag="pool_then_scale")
        table_blocks = table.rearrange("(b p) d -> p b d", p=P)
        nc.sync.dma_start(table_rows[:, 0:2, :], table_blocks[:, 0:2, :])
        nc.scalar.dma_start(table_rows[:, 2:4, :], table_blocks[:, 2:4, :])

        offsets = held.tile([P, N // 16], U16, name="offsets")
        nc.sync.dma_start(offsets[:], offs)
        q_cols = held.tile([D, M], BF16, name="q_cols")
        nc.sync.dma_start(q_cols[:], q)
        key_scale = held.tile([P, N], F32, name="key_scale")
        nc.scalar.dma_start(key_scale[:], k_scale.rearrange("o n -> (o n)").partition_broadcast(P))
        v_rows = held.tile([P, KEY_BLOCKS, D], BF16, name="v_rows")
        nc.sync.dma_start(v_rows[:], v.rearrange("(b p) e -> p b e", p=P))

        ahead = held.tile([P, P], F32, name="ahead")
        nc.gpsimd.iota(
            ahead[:], pattern=[[1, P]], base=0, channel_multiplier=-1, allow_small_or_imprecise_dtypes=True
        )

        warmed = held.tile([P, 1], F32, name="warmed")
        nc.vector.memset(warmed[:], 0.0)
        nc.scalar.activation(warmed[:], warmed[:], ACT.Exp)

        identity_f32 = held.tile([P, P], F32, name="identity_f32")
        nc.vector.tensor_scalar(out=identity_f32[:], in0=ahead[:], scalar1=0.0, scalar2=None, op0=ALU.is_equal)

        causal_bias = held.tile([P, P], F32, name="causal_bias")
        nc.vector.tensor_scalar(
            out=causal_bias[:], in0=ahead[:], scalar1=0.0, scalar2=MASKED, op0=ALU.is_gt, op1=ALU.mult
        )

        identity = held.tile([P, P], BF16, name="identity")
        nc.vector.tensor_scalar(out=identity[:], in0=ahead[:], scalar1=0.0, scalar2=None, op0=ALU.is_equal)

        steep = held.tile([P, P], F32, name="steep")
        nc.vector.tensor_scalar(
            out=steep[:], in0=ahead[:], scalar1=0.5, scalar2=STEEP, op0=ALU.subtract, op1=ALU.mult
        )

        keys = [(i + 1) * P for i in range(QUERY_BLOCKS)]
        order = list(reversed(range(QUERY_BLOCKS)))
        tiles = [(i, b) for i in order for b in range(i + 1)]

        scores_ps = {pair: score_psum.tile([P, P], F32, name="scores_ps") for pair in tiles}
        for i in order:
            nc.tensor.matmul(scores_ps[(i, i)][:], identity_f32[:], causal_bias[:], start=True, stop=False)

        table_cols = held.tile([D, S], BF16, name="table_cols")
        with tc.psum_pool(name="flip_psum", bufs=SLOT_BLOCKS) as flip_psum:
            for b in range(SLOT_BLOCKS):
                flipped = flip_psum.tile([D, P], BF16, name="flipped")
                nc.tensor.transpose(flipped[:], table_rows[:, b, :], identity[:])
                nc.vector.tensor_copy(table_cols[:, b * P : (b + 1) * P], flipped[:])

        seen_scale = shared.tile([P, N], F32, name="seen_scale", tag="pool_then_scale")
        nc.vector.scalar_tensor_tensor(
            out=seen_scale[:].rearrange("p (b j) -> p b j", j=P),
            in0=steep[:].unsqueeze(1).to_broadcast([P, KEY_BLOCKS, P]),
            scalar=1.0,
            in1=key_scale[:].rearrange("p (b j) -> p b j", j=P),
            op0=ALU.min,
            op1=ALU.max,
        )

        for i, b in tiles:
            nc.tensor.matmul(
                scores_ps[(i, b)][:],
                q_cols[:, i * P : (i + 1) * P],
                table_cols[:].indirect(offsets[:, b * P // 16 : (b + 1) * P // 16]),
                start=(b != i),
                stop=True,
            )

        scores = [work.tile([P, keys[i]], F32, name="scores") for i in range(QUERY_BLOCKS)]
        neg_max = [work.tile([P, 1], F32, name="neg_max") for i in range(QUERY_BLOCKS)]
        for i, b in tiles:
            tile_scale = seen_scale if b == i else key_scale
            nc.vector.scalar_tensor_tensor(
                out=scores[i][:, b * P : (b + 1) * P],
                in0=scores_ps[(i, b)][:],
                scalar=1.0 / math.sqrt(D),
                in1=tile_scale[:, b * P : (b + 1) * P],
                op0=ALU.mult,
                op1=ALU.mult,
            )
        for i in order:
            nc.vector.reduce_max(neg_max[i][:], scores[i][:], axis=mybir.AxisListType.X, negate=True)

        with (
            tc.psum_pool(name="flipped_psum", bufs=SCORE_TILES) as flipped_psum,
            tc.psum_pool(name="psum", bufs=QUERY_BLOCKS) as psum,
        ):
            for i in order:
                weights = work.tile([P, keys[i]], BF16, name="weights")
                row_sum = work.tile([P, 1], F32, name="row_sum")
                nc.scalar.activation(
                    weights[:], scores[i][:], ACT.Exp, bias=neg_max[i][:], scale=1.0, accum_out=row_sum[:]
                )
                inv_sum = work.tile([P, 1], F32, name="inv_sum")
                nc.vector.reciprocal(inv_sum[:], row_sum[:])

                weights_flipped = work.tile([P, keys[i]], BF16, name="weights_flipped")
                for b in range(i + 1):
                    weights_flipped_ps = flipped_psum.tile([P, P], BF16, name="weights_flipped_ps")
                    nc.tensor.transpose(weights_flipped_ps[:], weights[:, b * P : (b + 1) * P], identity[:])
                    nc.vector.tensor_copy(weights_flipped[:, b * P : (b + 1) * P], weights_flipped_ps[:])

                out_ps = psum.tile([P, D], F32, name="out_ps")
                for b in range(i + 1):
                    nc.tensor.matmul(
                        out_ps[:], weights_flipped[:, b * P : (b + 1) * P], v_rows[:, b, :], start=(b == 0), stop=(b == i)
                    )
                out_rows = work.tile([P, D], F32, name="out_rows")
                nc.vector.tensor_scalar_mul(out_rows[:], out_ps[:], inv_sum[:])
                nc.sync.dma_start(out[i * P : (i + 1) * P, :], out_rows[:])
